import numpy as np
import ml_dtypes

BF16 = ml_dtypes.bfloat16


def bf(x):
    return np.asarray(x, np.float32).astype(BF16)


def f32(x):
    return np.asarray(x, np.float32)


def f64(x):
    return np.asarray(x).astype(np.float64)


def striped(idx):
    return np.tile(idx.reshape(-1, 16).T, (8, 1))


C, S, N = 512, 2048, 256
BASE = 10000.0


def sinusoidal_pe():
    pos = np.arange(N, dtype=np.float32)[None, :]
    i = np.arange(C)[:, None]
    denom = np.power(np.float32(BASE), (2 * (i // 2)).astype(np.float32) / np.float32(C))
    angle = f64(pos / denom)
    return np.where(i % 2 == 0, np.sin(angle), np.cos(angle))


def setup_inputs():
    return {"emb": f32(np.random.standard_normal((C, S))), "pe": f32(sinusoidal_pe()), "offs": striped(np.random.permutation(np.tile(np.arange(S), 2))[:N])}


def reference(emb, pe, offs):
    idx = offs[:16].T.reshape(-1)
    return f64(emb)[:, idx] + f64(pe)

@@ -1,0 +1,28 @@
+import concourse.mybir as mybir
+
+F32 = mybir.dt.float32
+U16 = mybir.dt.uint16
+ADD = mybir.AluOpType.add
+
+P = 128
+FEATURES = 512
+WORDS = 2048
+TOKENS = 256
+BLOCKS = FEATURES // P
+
+
+def tile_word_embedding_kernel(tc, emb, pe, offs, out):
+    nc = tc.nc
+    with tc.tile_pool(name="held", bufs=1) as held:
+        offsets = held.tile([P, TOKENS // 16], U16, name="offsets")
+        nc.sync.dma_start(offsets[:], offs)
+
+        for b in range(BLOCKS):
+            rows = slice(b * P, (b + 1) * P)
+            table = held.tile([P, WORDS], F32, name=f"table{b}")
+            position = held.tile([P, TOKENS], F32, name=f"position{b}")
+            summed = held.tile([P, TOKENS], F32, name=f"summed{b}")
+            nc.sync.dma_start(table[:], emb[rows, :])
+            nc.scalar.dma_start(position[:], pe[rows, :])
+            nc.vector.tensor_tensor(summed[:], table[:].indirect(offsets[:]), position[:], ADD)
+            nc.scalar.dma_start(out[rows, :], summed[:])

@@ -25,4 +25,4 @@ def tile_word_embedding_kernel(tc, emb, pe, offs, out):
             nc.sync.dma_start(table[:], emb[rows, :])
             nc.scalar.dma_start(position[:], pe[rows, :])
             nc.vector.tensor_tensor(summed[:], table[:].indirect(offsets[:]), position[:], ADD)
-            nc.scalar.dma_start(out[rows, :], summed[:])
+            nc.sync.dma_start(out[rows, :], summed[:])

@@ -17,12 +17,21 @@ def tile_word_embedding_kernel(tc, emb, pe, offs, out):
         offsets = held.tile([P, TOKENS // 16], U16, name="offsets")
         nc.sync.dma_start(offsets[:], offs)
 
+        tables = []
+        positions = []
         for b in range(BLOCKS):
             rows = slice(b * P, (b + 1) * P)
             table = held.tile([P, WORDS], F32, name=f"table{b}")
             position = held.tile([P, TOKENS], F32, name=f"position{b}")
-            summed = held.tile([P, TOKENS], F32, name=f"summed{b}")
             nc.sync.dma_start(table[:], emb[rows, :])
             nc.scalar.dma_start(position[:], pe[rows, :])
-            nc.vector.tensor_tensor(summed[:], table[:].indirect(offsets[:]), position[:], ADD)
+            tables.append(table)
+            positions.append(position)
+
+        for b in range(BLOCKS):
+            rows = slice(b * P, (b + 1) * P)
+            summed = held.tile([P, TOKENS], F32, name=f"summed{b}")
+            nc.vector.tensor_tensor(
+                summed[:], tables[b][:].indirect(offsets[:]), positions[b][:], ADD
+            )
             nc.sync.dma_start(out[rows, :], summed[:])

@@ -13,25 +13,28 @@ BLOCKS = FEATURES // P
 
 def tile_word_embedding_kernel(tc, emb, pe, offs, out):
     nc = tc.nc
+    emb_blocks = emb.rearrange("(p b) w -> b p w", b=BLOCKS)
+    out_blocks = out.rearrange("(p b) j -> b p j", b=BLOCKS)
+    pe_rows = pe.rearrange("(p b) j -> p (b j)", b=BLOCKS)
+
     with tc.tile_pool(name="held", bufs=1) as held:
         offsets = held.tile([P, TOKENS // 16], U16, name="offsets")
         nc.sync.dma_start(offsets[:], offs)
 
+        position = held.tile([P, BLOCKS * TOKENS], F32, name="position")
+        nc.scalar.dma_start(position[:], pe_rows)
         tables = []
-        positions = []
         for b in range(BLOCKS):
-            rows = slice(b * P, (b + 1) * P)
             table = held.tile([P, WORDS], F32, name=f"table{b}")
-            position = held.tile([P, TOKENS], F32, name=f"position{b}")
-            nc.sync.dma_start(table[:], emb[rows, :])
-            nc.scalar.dma_start(position[:], pe[rows, :])
+            nc.sync.dma_start(table[:], emb_blocks[b])
             tables.append(table)
-            positions.append(position)
 
         for b in range(BLOCKS):
-            rows = slice(b * P, (b + 1) * P)
             summed = held.tile([P, TOKENS], F32, name=f"summed{b}")
             nc.vector.tensor_tensor(
-                summed[:], tables[b][:].indirect(offsets[:]), positions[b][:], ADD
+                summed[:],
+                tables[b][:].indirect(offsets[:]),
+                position[:, b * TOKENS : (b + 1) * TOKENS],
+                ADD,
             )
-            nc.sync.dma_start(out[rows, :], summed[:])
+            nc.sync.dma_start(out_blocks[b], summed[:])

@@ -9,6 +9,7 @@ FEATURES = 512
 WORDS = 2048
 TOKENS = 256
 BLOCKS = FEATURES // P
+HALF = WORDS // 2
 
 
 def tile_word_embedding_kernel(tc, emb, pe, offs, out):
@@ -26,7 +27,8 @@ def tile_word_embedding_kernel(tc, emb, pe, offs, out):
         tables = []
         for b in range(BLOCKS):
             table = held.tile([P, WORDS], F32, name=f"table{b}")
-            nc.sync.dma_start(table[:], emb_blocks[b])
+            nc.sync.dma_start(table[:, :HALF], emb_blocks[b][:, :HALF])
+            nc.scalar.dma_start(table[:, HALF:], emb_blocks[b][:, HALF:])
             tables.append(table)
 
         for b in range(BLOCKS):

@@ -9,7 +9,6 @@ FEATURES = 512
 WORDS = 2048
 TOKENS = 256
 BLOCKS = FEATURES // P
-HALF = WORDS // 2
 
 
 def tile_word_embedding_kernel(tc, emb, pe, offs, out):
@@ -23,12 +22,11 @@ def tile_word_embedding_kernel(tc, emb, pe, offs, out):
         nc.sync.dma_start(offsets[:], offs)
 
         position = held.tile([P, BLOCKS * TOKENS], F32, name="position")
-        nc.scalar.dma_start(position[:], pe_rows)
+        nc.sync.dma_start(position[:], pe_rows)
         tables = []
         for b in range(BLOCKS):
             table = held.tile([P, WORDS], F32, name=f"table{b}")
-            nc.sync.dma_start(table[:, :HALF], emb_blocks[b][:, :HALF])
-            nc.scalar.dma_start(table[:, HALF:], emb_blocks[b][:, HALF:])
+            nc.sync.dma_start(table[:], emb_blocks[b])
             tables.append(table)
 
         for b in range(BLOCKS):

@@ -14,8 +14,9 @@ BLOCKS = FEATURES // P
 def tile_word_embedding_kernel(tc, emb, pe, offs, out):
     nc = tc.nc
     emb_blocks = emb.rearrange("(p b) w -> b p w", b=BLOCKS)
-    out_blocks = out.rearrange("(p b) j -> b p j", b=BLOCKS)
+    out_rows = out.rearrange("(p b) j -> p (b j)", b=BLOCKS)
     pe_rows = pe.rearrange("(p b) j -> p (b j)", b=BLOCKS)
+    early = (BLOCKS - 1) * TOKENS
 
     with tc.tile_pool(name="held", bufs=1) as held:
         offsets = held.tile([P, TOKENS // 16], U16, name="offsets")
@@ -29,12 +30,18 @@ def tile_word_embedding_kernel(tc, emb, pe, offs, out):
             nc.sync.dma_start(table[:], emb_blocks[b])
             tables.append(table)
 
+        summed_early = held.tile([P, early], F32, name="summed_early")
+        summed_last = held.tile([P, TOKENS], F32, name="summed_last")
         for b in range(BLOCKS):
-            summed = held.tile([P, TOKENS], F32, name=f"summed{b}")
+            if b < BLOCKS - 1:
+                summed = summed_early[:, b * TOKENS : (b + 1) * TOKENS]
+            else:
+                summed = summed_last[:]
             nc.vector.tensor_tensor(
-                summed[:],
+                summed,
                 tables[b][:].indirect(offsets[:]),
                 position[:, b * TOKENS : (b + 1) * TOKENS],
                 ADD,
             )
-            nc.sync.dma_start(out_blocks[b], summed[:])
+        nc.sync.dma_start(out_rows[:, 0:early], summed_early[:])
+        nc.sync.dma_start(out_rows[:, early : early + TOKENS], summed_last[:])

@@ -20,15 +20,14 @@ def tile_word_embedding_kernel(tc, emb, pe, offs, out):
 
     with tc.tile_pool(name="held", bufs=1) as held:
         offsets = held.tile([P, TOKENS // 16], U16, name="offsets")
-        nc.sync.dma_start(offsets[:], offs)
-
         position = held.tile([P, BLOCKS * TOKENS], F32, name="position")
+        tables = [held.tile([P, WORDS], F32, name=f"table{b}") for b in range(BLOCKS)]
+
+        nc.sync.dma_start(tables[0][:], emb_blocks[0])
+        nc.sync.dma_start(offsets[:], offs)
         nc.sync.dma_start(position[:], pe_rows)
-        tables = []
-        for b in range(BLOCKS):
-            table = held.tile([P, WORDS], F32, name=f"table{b}")
-            nc.sync.dma_start(table[:], emb_blocks[b])
-            tables.append(table)
+        for b in range(1, BLOCKS):
+            nc.sync.dma_start(tables[b][:], emb_blocks[b])
 
         summed_early = held.tile([P, early], F32, name="summed_early")
         summed_last = held.tile([P, TOKENS], F32, name="summed_last")

@@ -9,6 +9,7 @@ FEATURES = 512
 WORDS = 2048
 TOKENS = 256
 BLOCKS = FEATURES // P
+AXI_BYTES = 256
 
 
 def tile_word_embedding_kernel(tc, emb, pe, offs, out):
@@ -20,8 +21,11 @@ def tile_word_embedding_kernel(tc, emb, pe, offs, out):
 
     with tc.tile_pool(name="held", bufs=1) as held:
         offsets = held.tile([P, TOKENS // 16], U16, name="offsets")
-        position = held.tile([P, BLOCKS * TOKENS], F32, name="position")
-        tables = [held.tile([P, WORDS], F32, name=f"table{b}") for b in range(BLOCKS)]
+        position = held.tile([P, BLOCKS * TOKENS], F32, name="position", align_bytes=AXI_BYTES)
+        tables = [
+            held.tile([P, WORDS], F32, name=f"table{b}", align_bytes=AXI_BYTES)
+            for b in range(BLOCKS)
+        ]
 
         nc.sync.dma_start(tables[0][:], emb_blocks[0])
         nc.sync.dma_start(offsets[:], offs)
@@ -29,8 +33,8 @@ def tile_word_embedding_kernel(tc, emb, pe, offs, out):
         for b in range(1, BLOCKS):
             nc.sync.dma_start(tables[b][:], emb_blocks[b])
 
-        summed_early = held.tile([P, early], F32, name="summed_early")
-        summed_last = held.tile([P, TOKENS], F32, name="summed_last")
+        summed_early = held.tile([P, early], F32, name="summed_early", align_bytes=AXI_BYTES)
+        summed_last = held.tile([P, TOKENS], F32, name="summed_last", align_bytes=AXI_BYTES)
         for b in range(BLOCKS):
             if b < BLOCKS - 1:
                 summed = summed_early[:, b * TOKENS : (b + 1) * TOKENS]

@@ -9,7 +9,7 @@ FEATURES = 512
 WORDS = 2048
 TOKENS = 256
 BLOCKS = FEATURES // P
-AXI_BYTES = 256
+PACKET_BYTES = 4096
 
 
 def tile_word_embedding_kernel(tc, emb, pe, offs, out):
@@ -21,9 +21,9 @@ def tile_word_embedding_kernel(tc, emb, pe, offs, out):
 
     with tc.tile_pool(name="held", bufs=1) as held:
         offsets = held.tile([P, TOKENS // 16], U16, name="offsets")
-        position = held.tile([P, BLOCKS * TOKENS], F32, name="position", align_bytes=AXI_BYTES)
+        position = held.tile([P, BLOCKS * TOKENS], F32, name="position", align_bytes=PACKET_BYTES)
         tables = [
-            held.tile([P, WORDS], F32, name=f"table{b}", align_bytes=AXI_BYTES)
+            held.tile([P, WORDS], F32, name=f"table{b}", align_bytes=PACKET_BYTES)
             for b in range(BLOCKS)
         ]
 
@@ -33,8 +33,8 @@ def tile_word_embedding_kernel(tc, emb, pe, offs, out):
         for b in range(1, BLOCKS):
             nc.sync.dma_start(tables[b][:], emb_blocks[b])
 
-        summed_early = held.tile([P, early], F32, name="summed_early", align_bytes=AXI_BYTES)
-        summed_last = held.tile([P, TOKENS], F32, name="summed_last", align_bytes=AXI_BYTES)
+        summed_early = held.tile([P, early], F32, name="summed_early", align_bytes=PACKET_BYTES)
+        summed_last = held.tile([P, TOKENS], F32, name="summed_last", align_bytes=PACKET_BYTES)
         for b in range(BLOCKS):
             if b < BLOCKS - 1:
                 summed = summed_early[:, b * TOKENS : (b + 1) * TOKENS]

@@ -9,6 +9,8 @@ FEATURES = 512
 WORDS = 2048
 TOKENS = 256
 BLOCKS = FEATURES // P
+HALF = TOKENS // 2
+HALF_COLUMNS = HALF // 16
 PACKET_BYTES = 4096
 
 
@@ -17,34 +19,53 @@ def tile_word_embedding_kernel(tc, emb, pe, offs, out):
     emb_blocks = emb.rearrange("(p b) w -> b p w", b=BLOCKS)
     out_rows = out.rearrange("(p b) j -> p (b j)", b=BLOCKS)
     pe_rows = pe.rearrange("(p b) j -> p (b j)", b=BLOCKS)
-    early = (BLOCKS - 1) * TOKENS
+    last = BLOCKS - 1
+    early = last * TOKENS
+    middle = early + HALF
 
     with tc.tile_pool(name="held", bufs=1) as held:
         offsets = held.tile([P, TOKENS // 16], U16, name="offsets")
-        position = held.tile([P, BLOCKS * TOKENS], F32, name="position", align_bytes=PACKET_BYTES)
         tables = [
             held.tile([P, WORDS], F32, name=f"table{b}", align_bytes=PACKET_BYTES)
             for b in range(BLOCKS)
         ]
+        position_early = held.tile([P, early], F32, name="position_early", align_bytes=PACKET_BYTES)
+        position_middle = held.tile([P, HALF], F32, name="position_middle", align_bytes=PACKET_BYTES)
+        position_end = held.tile([P, HALF], F32, name="position_end", align_bytes=PACKET_BYTES)
+        summed_early = held.tile([P, early], F32, name="summed_early", align_bytes=PACKET_BYTES)
+        summed_middle = held.tile([P, HALF], F32, name="summed_middle", align_bytes=PACKET_BYTES)
+        summed_end = held.tile([P, HALF], F32, name="summed_end", align_bytes=PACKET_BYTES)
 
         nc.sync.dma_start(tables[0][:], emb_blocks[0])
         nc.sync.dma_start(offsets[:], offs)
-        nc.sync.dma_start(position[:], pe_rows)
-        for b in range(1, BLOCKS):
+        nc.sync.dma_start(position_early[:], pe_rows[:, 0:early])
+        for b in range(1, last):
             nc.sync.dma_start(tables[b][:], emb_blocks[b])
+        nc.sync.dma_start(position_middle[:], pe_rows[:, early:middle])
+        nc.sync.dma_start(tables[last][:], emb_blocks[last])
+        nc.sync.dma_start(position_end[:], pe_rows[:, middle:])
 
-        summed_early = held.tile([P, early], F32, name="summed_early", align_bytes=PACKET_BYTES)
-        summed_last = held.tile([P, TOKENS], F32, name="summed_last", align_bytes=PACKET_BYTES)
-        for b in range(BLOCKS):
-            if b < BLOCKS - 1:
-                summed = summed_early[:, b * TOKENS : (b + 1) * TOKENS]
-            else:
-                summed = summed_last[:]
+        for b in range(last):
+            columns = slice(b * TOKENS, (b + 1) * TOKENS)
             nc.vector.tensor_tensor(
-                summed,
+                summed_early[:, columns],
                 tables[b][:].indirect(offsets[:]),
-                position[:, b * TOKENS : (b + 1) * TOKENS],
+                position_early[:, columns],
                 ADD,
             )
         nc.sync.dma_start(out_rows[:, 0:early], summed_early[:])
-        nc.sync.dma_start(out_rows[:, early : early + TOKENS], summed_last[:])
+
+        nc.vector.tensor_tensor(
+            summed_middle[:],
+            tables[last][:].indirect(offsets[:, 0:HALF_COLUMNS]),
+            position_middle[:],
+            ADD,
+        )
+        nc.sync.dma_start(out_rows[:, early:middle], summed_middle[:])
+        nc.vector.tensor_tensor(
+            summed_end[:],
+            tables[last][:].indirect(offsets[:, HALF_COLUMNS:]),
+            position_end[:],
+            ADD,
+        )
+        nc.sync.dma_start(out_rows[:, middle:], summed_end[:])

@@ -19,9 +19,8 @@ def tile_word_embedding_kernel(tc, emb, pe, offs, out):
     emb_blocks = emb.rearrange("(p b) w -> b p w", b=BLOCKS)
     out_rows = out.rearrange("(p b) j -> p (b j)", b=BLOCKS)
     pe_rows = pe.rearrange("(p b) j -> p (b j)", b=BLOCKS)
-    last = BLOCKS - 1
-    early = last * TOKENS
-    middle = early + HALF
+    cuts = [0, 4 * HALF, 7 * HALF, 8 * HALF]
+    pieces = [slice(cuts[i], cuts[i + 1]) for i in range(3)]
 
     with tc.tile_pool(name="held", bufs=1) as held:
         offsets = held.tile([P, TOKENS // 16], U16, name="offsets")
@@ -29,43 +28,31 @@ def tile_word_embedding_kernel(tc, emb, pe, offs, out):
             held.tile([P, WORDS], F32, name=f"table{b}", align_bytes=PACKET_BYTES)
             for b in range(BLOCKS)
         ]
-        position_early = held.tile([P, early], F32, name="position_early", align_bytes=PACKET_BYTES)
-        position_middle = held.tile([P, HALF], F32, name="position_middle", align_bytes=PACKET_BYTES)
-        position_end = held.tile([P, HALF], F32, name="position_end", align_bytes=PACKET_BYTES)
-        summed_early = held.tile([P, early], F32, name="summed_early", align_bytes=PACKET_BYTES)
-        summed_middle = held.tile([P, HALF], F32, name="summed_middle", align_bytes=PACKET_BYTES)
-        summed_end = held.tile([P, HALF], F32, name="summed_end", align_bytes=PACKET_BYTES)
+        positions = [
+            held.tile([P, cuts[i + 1] - cuts[i]], F32, name=f"position{i}", align_bytes=PACKET_BYTES)
+            for i in range(3)
+        ]
 
         nc.sync.dma_start(tables[0][:], emb_blocks[0])
         nc.sync.dma_start(offsets[:], offs)
-        nc.sync.dma_start(position_early[:], pe_rows[:, 0:early])
-        for b in range(1, last):
-            nc.sync.dma_start(tables[b][:], emb_blocks[b])
-        nc.sync.dma_start(position_middle[:], pe_rows[:, early:middle])
-        nc.sync.dma_start(tables[last][:], emb_blocks[last])
-        nc.sync.dma_start(position_end[:], pe_rows[:, middle:])
+        nc.sync.dma_start(positions[0][:], pe_rows[:, pieces[0]])
+        nc.sync.dma_start(tables[1][:], emb_blocks[1])
+        nc.sync.dma_start(positions[1][:], pe_rows[:, pieces[1]])
+        nc.sync.dma_start(tables[2][:], emb_blocks[2])
+        nc.sync.dma_start(tables[3][:], emb_blocks[3])
+        nc.sync.dma_start(positions[2][:], pe_rows[:, pieces[2]])
 
-        for b in range(last):
-            columns = slice(b * TOKENS, (b + 1) * TOKENS)
+        for half in range(2 * BLOCKS):
+            block, part = divmod(half, 2)
+            piece = 0 if half < 4 else 1 if half < 7 else 2
+            start = half * HALF
+            summed = held.tile([P, HALF], F32, name=f"summed{half}", align_bytes=PACKET_BYTES)
             nc.vector.tensor_tensor(
-                summed_early[:, columns],
-                tables[b][:].indirect(offsets[:]),
-                position_early[:, columns],
+                summed[:],
+                tables[block][:].indirect(
+                    offsets[:, part * HALF_COLUMNS : (part + 1) * HALF_COLUMNS]
+                ),
+                positions[piece][:, start - cuts[piece] : start - cuts[piece] + HALF],
                 ADD,
             )
-        nc.sync.dma_start(out_rows[:, 0:early], summed_early[:])
-
-        nc.vector.tensor_tensor(
-            summed_middle[:],
-            tables[last][:].indirect(offsets[:, 0:HALF_COLUMNS]),
-            position_middle[:],
-            ADD,
-        )
-        nc.sync.dma_start(out_rows[:, early:middle], summed_middle[:])
-        nc.vector.tensor_tensor(
-            summed_end[:],
-            tables[last][:].indirect(offsets[:, HALF_COLUMNS:]),
-            position_end[:],
-            ADD,
-        )
-        nc.sync.dma_start(out_rows[:, middle:], summed_end[:])
+            nc.sync.dma_start(out_rows[:, start : start + HALF], summed[:])

@@ -9,6 +9,7 @@ FEATURES = 512
 WORDS = 2048
 TOKENS = 256
 BLOCKS = FEATURES // P
+PAIR = 2
 HALF = TOKENS // 2
 HALF_COLUMNS = HALF // 16
 PACKET_BYTES = 4096
@@ -16,11 +17,12 @@ PACKET_BYTES = 4096
 
 def tile_word_embedding_kernel(tc, emb, pe, offs, out):
     nc = tc.nc
-    emb_blocks = emb.rearrange("(p b) w -> b p w", b=BLOCKS)
-    out_rows = out.rearrange("(p b) j -> p (b j)", b=BLOCKS)
-    pe_rows = pe.rearrange("(p b) j -> p (b j)", b=BLOCKS)
-    cuts = [0, 4 * HALF, 7 * HALF, 8 * HALF]
-    pieces = [slice(cuts[i], cuts[i + 1]) for i in range(3)]
+    emb_blocks = emb.rearrange("(h p b) w -> h b p w", p=P, b=PAIR)
+    out_rows = out.rearrange("(h p b) j -> h p (b j)", p=P, b=PAIR)
+    pe_rows = pe.rearrange("(h p b) j -> h p (b j)", p=P, b=PAIR)
+    late = (2 * PAIR - 1) * HALF
+    sources = [pe_rows[0], pe_rows[1][:, 0:late], pe_rows[1][:, late:]]
+    widths = [PAIR * TOKENS, late, HALF]
 
     with tc.tile_pool(name="held", bufs=1) as held:
         offsets = held.tile([P, TOKENS // 16], U16, name="offsets")
@@ -29,30 +31,36 @@ def tile_word_embedding_kernel(tc, emb, pe, offs, out):
             for b in range(BLOCKS)
         ]
         positions = [
-            held.tile([P, cuts[i + 1] - cuts[i]], F32, name=f"position{i}", align_bytes=PACKET_BYTES)
+            held.tile([P, widths[i]], F32, name=f"position{i}", align_bytes=PACKET_BYTES)
             for i in range(3)
         ]
 
-        nc.sync.dma_start(tables[0][:], emb_blocks[0])
+        nc.sync.dma_start(tables[0][:], emb_blocks[0][0])
         nc.sync.dma_start(offsets[:], offs)
-        nc.sync.dma_start(positions[0][:], pe_rows[:, pieces[0]])
-        nc.sync.dma_start(tables[1][:], emb_blocks[1])
-        nc.sync.dma_start(positions[1][:], pe_rows[:, pieces[1]])
-        nc.sync.dma_start(tables[2][:], emb_blocks[2])
-        nc.sync.dma_start(tables[3][:], emb_blocks[3])
-        nc.sync.dma_start(positions[2][:], pe_rows[:, pieces[2]])
+        nc.sync.dma_start(positions[0][:], sources[0])
+        nc.sync.dma_start(tables[1][:], emb_blocks[0][1])
+        nc.sync.dma_start(positions[1][:], sources[1])
+        nc.sync.dma_start(tables[2][:], emb_blocks[1][0])
+        nc.sync.dma_start(tables[3][:], emb_blocks[1][1])
+        nc.sync.dma_start(positions[2][:], sources[2])
 
         for half in range(2 * BLOCKS):
             block, part = divmod(half, 2)
-            piece = 0 if half < 4 else 1 if half < 7 else 2
-            start = half * HALF
+            pair, place = divmod(half, 2 * PAIR)
+            start = place * HALF
+            if pair == 0:
+                added = positions[0][:, start : start + HALF]
+            elif start < late:
+                added = positions[1][:, start : start + HALF]
+            else:
+                added = positions[2][:]
             summed = held.tile([P, HALF], F32, name=f"summed{half}", align_bytes=PACKET_BYTES)
             nc.vector.tensor_tensor(
                 summed[:],
                 tables[block][:].indirect(
                     offsets[:, part * HALF_COLUMNS : (part + 1) * HALF_COLUMNS]
                 ),
-                positions[piece][:, start - cuts[piece] : start - cuts[piece] + HALF],
+                added,
                 ADD,
             )
-            nc.sync.dma_start(out_rows[:, start : start + HALF], summed[:])
+            nc.sync.dma_start(out_rows[pair][:, start : start + HALF], summed[:])

import concourse.mybir as mybir

F32 = mybir.dt.float32
U16 = mybir.dt.uint16
ADD = mybir.AluOpType.add

P = 128
FEATURES = 512
WORDS = 2048
TOKENS = 256
BLOCKS = FEATURES // P
PAIR = 2
HALF = TOKENS // 2
HALF_COLUMNS = HALF // 16
PACKET_BYTES = 4096


def tile_word_embedding_kernel(tc, emb, pe, offs, out):
    nc = tc.nc
    emb_blocks = emb.rearrange("(h p b) w -> h b p w", p=P, b=PAIR)
    out_rows = out.rearrange("(h p b) j -> h p (b j)", p=P, b=PAIR)
    pe_rows = pe.rearrange("(h p b) j -> h p (b j)", p=P, b=PAIR)
    late = (2 * PAIR - 1) * HALF
    sources = [pe_rows[0], pe_rows[1][:, 0:late], pe_rows[1][:, late:]]
    widths = [PAIR * TOKENS, late, HALF]

    with tc.tile_pool(name="held", bufs=1) as held:
        offsets = held.tile([P, TOKENS // 16], U16, name="offsets")
        tables = [
            held.tile([P, WORDS], F32, name=f"table{b}", align_bytes=PACKET_BYTES)
            for b in range(BLOCKS)
        ]
        positions = [
            held.tile([P, widths[i]], F32, name=f"position{i}", align_bytes=PACKET_BYTES)
            for i in range(3)
        ]

        nc.sync.dma_start(tables[0][:], emb_blocks[0][0])
        nc.sync.dma_start(offsets[:], offs)
        nc.sync.dma_start(positions[0][:], sources[0])
        nc.sync.dma_start(tables[1][:], emb_blocks[0][1])
        nc.sync.dma_start(positions[1][:], sources[1])
        nc.sync.dma_start(tables[2][:], emb_blocks[1][0])
        nc.sync.dma_start(tables[3][:], emb_blocks[1][1])
        nc.sync.dma_start(positions[2][:], sources[2])

        for half in range(2 * BLOCKS):
            block, part = divmod(half, 2)
            pair, place = divmod(half, 2 * PAIR)
            start = place * HALF
            if pair == 0:
                added = positions[0][:, start : start + HALF]
            elif start < late:
                added = positions[1][:, start : start + HALF]
            else:
                added = positions[2][:]
            summed = held.tile([P, HALF], F32, name=f"summed{half}", align_bytes=PACKET_BYTES)
            nc.vector.tensor_tensor(
                summed[:],
                tables[block][:].indirect(
                    offsets[:, part * HALF_COLUMNS : (part + 1) * HALF_COLUMNS]
                ),
                added,
                ADD,
            )
            nc.sync.dma_start(out_rows[pair][:, start : start + HALF], summed[:])
